import numpy as np
import ml_dtypes

BF16 = ml_dtypes.bfloat16


def bf(x):
    return np.asarray(x, np.float32).astype(BF16)


def f32(x):
    return np.asarray(x, np.float32)


def f64(x):
    return np.asarray(x).astype(np.float64)


def striped(idx):
    return np.tile(idx.reshape(-1, 16).T, (8, 1))


H, Q, S, N = 128, 512, 1024, 512


def sigmoid(v):
    return 1.0 / (1.0 + np.exp(-v))


def setup_inputs():
    return {
        "table": bf(np.random.standard_normal((H, S))),
        "w_emb": bf(np.random.standard_normal((H, H)) / np.sqrt(H)),
        "ctx": f32(np.random.standard_normal((H, N))),
        "b_in": f32(0.2 * np.random.standard_normal((H, 1))),
        "w_ih": bf(np.random.standard_normal((H, Q)) / np.sqrt(H)),
        "w_hh": bf(np.random.standard_normal((H, Q)) / np.sqrt(H)),
        "h_prev": bf(np.random.standard_normal((H, N))),
        "c_prev": f32(np.random.standard_normal((H, N))),
        "b_lstm": f32(0.2 * np.random.standard_normal((Q, 1))),
        "offs": striped(np.random.permutation(np.tile(np.arange(S), 2))[:N]),
    }


def reference(table, w_emb, ctx, b_in, w_ih, w_hh, h_prev, c_prev, b_lstm, offs):
    idx = offs[:16].T.reshape(-1)
    x = f64(w_emb).T @ f64(table)[:, idx] + f64(ctx) + f64(b_in)
    z = f64(w_ih).T @ x + f64(w_hh).T @ f64(h_prev) + f64(b_lstm)
    zi, zf, zu, zo = z.reshape(-1, H, N)
    c = sigmoid(zf) * f64(c_prev) + sigmoid(zi) * np.tanh(zu)
    return sigmoid(zo) * np.tanh(c)

@@ -1,0 +1,85 @@
+import concourse.mybir as mybir
+
+BF16, F32, U16 = mybir.dt.bfloat16, mybir.dt.float32, mybir.dt.uint16
+ADD, MULT = mybir.AluOpType.add, mybir.AluOpType.mult
+SIGMOID = mybir.ActivationFunctionType.Sigmoid
+TANH = mybir.ActivationFunctionType.Tanh
+
+H = 128
+S = 1024
+N = 512
+GATES = ("i", "f", "u", "o")
+
+FLOPS = 2 * H * H * N + 2 * 2 * H * (4 * H) * N
+
+
+def tile_arrdecodermodel_kernel(
+    tc, table, w_emb, ctx, b_in, w_ih, w_hh, h_prev, c_prev, b_lstm, offs, out
+):
+    nc = tc.nc
+    with (
+        tc.tile_pool(name="held", bufs=1) as held,
+        tc.psum_pool(name="psum", bufs=1) as psum,
+    ):
+        offsets = held.tile([H, N // 16], U16, name="offsets")
+        nc.sync.dma_start(offsets[:], offs)
+        table_sb = held.tile([H, S], BF16, name="table_sb")
+        nc.sync.dma_start(table_sb[:], table)
+        w_emb_sb = held.tile([H, H], BF16, name="w_emb_sb")
+        nc.scalar.dma_start(w_emb_sb[:], w_emb)
+        w_hh_sb = held.tile([H, 4 * H], BF16, name="w_hh_sb")
+        nc.scalar.dma_start(w_hh_sb[:], w_hh)
+        h_prev_sb = held.tile([H, N], BF16, name="h_prev_sb")
+        nc.scalar.dma_start(h_prev_sb[:], h_prev)
+        ctx_sb = held.tile([H, N], F32, name="ctx_sb")
+        nc.sync.dma_start(ctx_sb[:], ctx)
+        w_ih_sb = held.tile([H, 4 * H], BF16, name="w_ih_sb")
+        nc.scalar.dma_start(w_ih_sb[:], w_ih)
+        c_prev_sb = held.tile([H, N], F32, name="c_prev_sb")
+        nc.sync.dma_start(c_prev_sb[:], c_prev)
+        b_in_sb = held.tile([H, 1], F32, name="b_in_sb")
+        nc.gpsimd.dma_start(b_in_sb[:], b_in)
+        b_lstm_sb = held.tile([H, 4], F32, name="b_lstm_sb")
+        with nc.allow_non_contiguous_dma(reason="512 bias values, one to a partition and gate"):
+            nc.gpsimd.dma_start(b_lstm_sb[:], b_lstm.rearrange("(g p) one -> p (g one)", p=H))
+
+        x_ps = psum.tile([H, N], F32, name="x_ps")
+        nc.tensor.matmul(
+            x_ps[:], w_emb_sb[:], table_sb[:].indirect(offsets[:]), start=True, stop=True
+        )
+
+        z_ps = {}
+        for g, gate in enumerate(GATES):
+            z_ps[gate] = psum.tile([H, N], F32, name=f"z_{gate}")
+            nc.tensor.matmul(
+                z_ps[gate][:], w_hh_sb[:, g * H : (g + 1) * H], h_prev_sb[:], start=True, stop=False
+            )
+
+        x_sb = held.tile([H, N], BF16, name="x_sb")
+        nc.vector.scalar_tensor_tensor(x_sb[:], x_ps[:], b_in_sb[:], ctx_sb[:], ADD, ADD)
+
+        for g, gate in enumerate(GATES):
+            nc.tensor.matmul(
+                z_ps[gate][:], w_ih_sb[:, g * H : (g + 1) * H], x_sb[:], start=False, stop=True
+            )
+
+        act = {}
+        for g, gate in enumerate(GATES):
+            act[gate] = held.tile([H, N], F32, name=f"act_{gate}")
+            nc.scalar.activation(
+                act[gate][:],
+                z_ps[gate][:],
+                TANH if gate == "u" else SIGMOID,
+                bias=b_lstm_sb[:, g : g + 1],
+            )
+        kept = held.tile([H, N], F32, name="kept")
+        nc.vector.tensor_tensor(kept[:], act["f"][:], c_prev_sb[:], MULT)
+        fresh = held.tile([H, N], F32, name="fresh")
+        nc.vector.tensor_tensor(fresh[:], act["i"][:], act["u"][:], MULT)
+        c_sb = held.tile([H, N], F32, name="c_sb")
+        nc.vector.tensor_tensor(c_sb[:], kept[:], fresh[:], ADD)
+        tanh_c = held.tile([H, N], F32, name="tanh_c")
+        nc.scalar.activation(tanh_c[:], c_sb[:], TANH)
+        out_sb = held.tile([H, N], F32, name="out_sb")
+        nc.vector.tensor_tensor(out_sb[:], act["o"][:], tanh_c[:], MULT)
+        nc.sync.dma_start(out, out_sb[:])

@@ -25,8 +25,13 @@ def tile_arrdecodermodel_kernel(
         nc.sync.dma_start(offsets[:], offs)
         table_sb = held.tile([H, S], BF16, name="table_sb")
         nc.sync.dma_start(table_sb[:], table)
+        b_in_sb = held.tile([H, 1], F32, name="b_in_sb")
+        nc.sync.dma_start(b_in_sb[:], b_in)
         w_emb_sb = held.tile([H, H], BF16, name="w_emb_sb")
         nc.scalar.dma_start(w_emb_sb[:], w_emb)
+        b_lstm_sb = held.tile([H, 4], F32, name="b_lstm_sb")
+        with nc.allow_non_contiguous_dma(reason="512 bias values, one to a partition and gate"):
+            nc.scalar.dma_start(b_lstm_sb[:], b_lstm.rearrange("(g p) one -> p (g one)", p=H))
         w_hh_sb = held.tile([H, 4 * H], BF16, name="w_hh_sb")
         nc.scalar.dma_start(w_hh_sb[:], w_hh)
         h_prev_sb = held.tile([H, N], BF16, name="h_prev_sb")
@@ -37,11 +42,10 @@ def tile_arrdecodermodel_kernel(
         nc.scalar.dma_start(w_ih_sb[:], w_ih)
         c_prev_sb = held.tile([H, N], F32, name="c_prev_sb")
         nc.sync.dma_start(c_prev_sb[:], c_prev)
-        b_in_sb = held.tile([H, 1], F32, name="b_in_sb")
-        nc.gpsimd.dma_start(b_in_sb[:], b_in)
-        b_lstm_sb = held.tile([H, 4], F32, name="b_lstm_sb")
-        with nc.allow_non_contiguous_dma(reason="512 bias values, one to a partition and gate"):
-            nc.gpsimd.dma_start(b_lstm_sb[:], b_lstm.rearrange("(g p) one -> p (g one)", p=H))
+
+        scratch = held.tile([H, 1], F32, name="scratch")
+        nc.gpsimd.memset(scratch[:], 0.0)
+        nc.scalar.activation(scratch[:], scratch[:], SIGMOID)
 
         x_ps = psum.tile([H, N], F32, name="x_ps")
         nc.tensor.matmul(

@@ -9,6 +9,7 @@ H = 128
 S = 1024
 N = 512
 GATES = ("i", "f", "u", "o")
+WARM_MATMULS = 6
 
 FLOPS = 2 * H * H * N + 2 * 2 * H * (4 * H) * N
 
@@ -46,6 +47,12 @@ def tile_arrdecodermodel_kernel(
         scratch = held.tile([H, 1], F32, name="scratch")
         nc.gpsimd.memset(scratch[:], 0.0)
         nc.scalar.activation(scratch[:], scratch[:], SIGMOID)
+
+        zeros = held.tile([H, N], BF16, name="zeros")
+        nc.vector.memset(zeros[:], 0.0)
+        warm_ps = psum.tile([H, N], F32, name="warm_ps")
+        for w in range(WARM_MATMULS):
+            nc.tensor.matmul(warm_ps[:], zeros[:, 0:H], zeros[:], start=True, stop=True)
 
         x_ps = psum.tile([H, N], F32, name="x_ps")
         nc.tensor.matmul(

@@ -8,8 +8,11 @@ TANH = mybir.ActivationFunctionType.Tanh
 H = 128
 S = 1024
 N = 512
+CHUNKS = 2
+W = N // CHUNKS
 GATES = ("i", "f", "u", "o")
-WARM_MATMULS = 6
+PSUM_BANKS = 8
+WARM_MATMULS = 16
 
 FLOPS = 2 * H * H * N + 2 * 2 * H * (4 * H) * N
 
@@ -20,77 +23,88 @@ def tile_arrdecodermodel_kernel(
     nc = tc.nc
     with (
         tc.tile_pool(name="held", bufs=1) as held,
-        tc.psum_pool(name="psum", bufs=1) as psum,
+        tc.tile_pool(name="work", bufs=CHUNKS) as work,
+        tc.psum_pool(name="psum", bufs=PSUM_BANKS) as psum,
     ):
-        offsets = held.tile([H, N // 16], U16, name="offsets")
-        nc.sync.dma_start(offsets[:], offs)
-        table_sb = held.tile([H, S], BF16, name="table_sb")
-        nc.sync.dma_start(table_sb[:], table)
-        b_in_sb = held.tile([H, 1], F32, name="b_in_sb")
-        nc.sync.dma_start(b_in_sb[:], b_in)
-        w_emb_sb = held.tile([H, H], BF16, name="w_emb_sb")
-        nc.scalar.dma_start(w_emb_sb[:], w_emb)
-        b_lstm_sb = held.tile([H, 4], F32, name="b_lstm_sb")
-        with nc.allow_non_contiguous_dma(reason="512 bias values, one to a partition and gate"):
-            nc.scalar.dma_start(b_lstm_sb[:], b_lstm.rearrange("(g p) one -> p (g one)", p=H))
-        w_hh_sb = held.tile([H, 4 * H], BF16, name="w_hh_sb")
-        nc.scalar.dma_start(w_hh_sb[:], w_hh)
-        h_prev_sb = held.tile([H, N], BF16, name="h_prev_sb")
-        nc.scalar.dma_start(h_prev_sb[:], h_prev)
-        ctx_sb = held.tile([H, N], F32, name="ctx_sb")
-        nc.sync.dma_start(ctx_sb[:], ctx)
-        w_ih_sb = held.tile([H, 4 * H], BF16, name="w_ih_sb")
-        nc.scalar.dma_start(w_ih_sb[:], w_ih)
-        c_prev_sb = held.tile([H, N], F32, name="c_prev_sb")
-        nc.sync.dma_start(c_prev_sb[:], c_prev)
-
+        zeros = held.tile([H, H], BF16, name="zeros")
+        nc.gpsimd.memset(zeros[:], 0.0)
         scratch = held.tile([H, 1], F32, name="scratch")
         nc.gpsimd.memset(scratch[:], 0.0)
+
+        b_in_sb = held.tile([H, 1], F32, name="b_in_sb")
+        nc.scalar.dma_start(b_in_sb[:], b_in)
+        b_lstm_sb = held.tile([H, 4], F32, name="b_lstm_sb")
+        with nc.allow_non_contiguous_dma(reason="512 bias values, one to a partition and gate"):
+            nc.gpsimd.dma_start(b_lstm_sb[:], b_lstm.rearrange("(g p) one -> p (g one)", p=H))
+
+        warm_ps = psum.tile([H, H], F32, name="warm_ps", tag="bank")
+        for w in range(WARM_MATMULS):
+            nc.tensor.matmul(warm_ps[:], zeros[:], zeros[:], start=True, stop=True)
+
         nc.scalar.activation(scratch[:], scratch[:], SIGMOID)
 
-        zeros = held.tile([H, N], BF16, name="zeros")
-        nc.vector.memset(zeros[:], 0.0)
-        warm_ps = psum.tile([H, N], F32, name="warm_ps")
-        for w in range(WARM_MATMULS):
-            nc.tensor.matmul(warm_ps[:], zeros[:, 0:H], zeros[:], start=True, stop=True)
+        offsets = held.tile([H, N // 16], U16, name="offsets")
+        nc.sync.dma_start(offsets[:], offs)
+        w_emb_sb = held.tile([H, H], BF16, name="w_emb_sb")
+        nc.sync.dma_start(w_emb_sb[:], w_emb)
+        table_sb = held.tile([H, S], BF16, name="table_sb")
+        nc.sync.dma_start(table_sb[:], table)
+        ctx_sb = [held.tile([H, W], F32, name=f"ctx_sb{c}") for c in range(CHUNKS)]
+        h_prev_sb = [held.tile([H, W], BF16, name=f"h_prev_sb{c}") for c in range(CHUNKS)]
+        w_hh_sb = held.tile([H, 4 * H], BF16, name="w_hh_sb")
+        w_ih_sb = held.tile([H, 4 * H], BF16, name="w_ih_sb")
+        c_prev_sb = held.tile([H, N], F32, name="c_prev_sb")
+        nc.sync.dma_start(ctx_sb[0][:], ctx[:, 0:W])
+        nc.sync.dma_start(h_prev_sb[0][:], h_prev[:, 0:W])
+        nc.sync.dma_start(w_hh_sb[:], w_hh)
+        nc.sync.dma_start(w_ih_sb[:], w_ih)
+        for c in range(1, CHUNKS):
+            nc.sync.dma_start(ctx_sb[c][:], ctx[:, c * W : (c + 1) * W])
+            nc.sync.dma_start(h_prev_sb[c][:], h_prev[:, c * W : (c + 1) * W])
+        nc.sync.dma_start(c_prev_sb[:], c_prev)
 
-        x_ps = psum.tile([H, N], F32, name="x_ps")
-        nc.tensor.matmul(
-            x_ps[:], w_emb_sb[:], table_sb[:].indirect(offsets[:]), start=True, stop=True
-        )
-
-        z_ps = {}
-        for g, gate in enumerate(GATES):
-            z_ps[gate] = psum.tile([H, N], F32, name=f"z_{gate}")
+        x_sb = []
+        for c in range(CHUNKS):
+            x_ps = psum.tile([H, W], F32, name="x_ps", tag="bank")
+            piece = offsets[:, c * (W // 16) : (c + 1) * (W // 16)]
             nc.tensor.matmul(
-                z_ps[gate][:], w_hh_sb[:, g * H : (g + 1) * H], h_prev_sb[:], start=True, stop=False
+                x_ps[:], w_emb_sb[:], table_sb[:].indirect(piece), start=True, stop=True
             )
+            x_sb.append(work.tile([H, W], BF16, name="x_sb"))
+            nc.vector.scalar_tensor_tensor(x_sb[c][:], x_ps[:], b_in_sb[:], ctx_sb[c][:], ADD, ADD)
 
-        x_sb = held.tile([H, N], BF16, name="x_sb")
-        nc.vector.scalar_tensor_tensor(x_sb[:], x_ps[:], b_in_sb[:], ctx_sb[:], ADD, ADD)
+        act_o = []
+        c_new = []
+        for c in range(CHUNKS):
+            z_ps = {}
+            for g, gate in enumerate(GATES):
+                z_ps[gate] = psum.tile([H, W], F32, name=f"z_{gate}", tag="bank")
+                nc.tensor.matmul(
+                    z_ps[gate][:], w_hh_sb[:, g * H : (g + 1) * H], h_prev_sb[c][:],
+                    start=True, stop=False,
+                )
+            act = {}
+            for g, gate in enumerate(GATES):
+                nc.tensor.matmul(
+                    z_ps[gate][:], w_ih_sb[:, g * H : (g + 1) * H], x_sb[c][:],
+                    start=False, stop=True,
+                )
+                act[gate] = work.tile([H, W], F32, name=f"act_{gate}")
+                nc.scalar.activation(
+                    act[gate][:], z_ps[gate][:], TANH if gate == "u" else SIGMOID,
+                    bias=b_lstm_sb[:, g : g + 1],
+                )
+            kept = work.tile([H, W], F32, name="kept")
+            nc.vector.tensor_tensor(kept[:], act["f"][:], c_prev_sb[:, c * W : (c + 1) * W], MULT)
+            fresh = work.tile([H, W], F32, name="fresh")
+            nc.vector.tensor_tensor(fresh[:], act["i"][:], act["u"][:], MULT)
+            c_new.append(work.tile([H, W], F32, name="c_new"))
+            nc.vector.tensor_tensor(c_new[c][:], kept[:], fresh[:], ADD)
+            act_o.append(act["o"])
 
-        for g, gate in enumerate(GATES):
-            nc.tensor.matmul(
-                z_ps[gate][:], w_ih_sb[:, g * H : (g + 1) * H], x_sb[:], start=False, stop=True
-            )
-
-        act = {}
-        for g, gate in enumerate(GATES):
-            act[gate] = held.tile([H, N], F32, name=f"act_{gate}")
-            nc.scalar.activation(
-                act[gate][:],
-                z_ps[gate][:],
-                TANH if gate == "u" else SIGMOID,
-                bias=b_lstm_sb[:, g : g + 1],
-            )
-        kept = held.tile([H, N], F32, name="kept")
-        nc.vector.tensor_tensor(kept[:], act["f"][:], c_prev_sb[:], MULT)
-        fresh = held.tile([H, N], F32, name="fresh")
-        nc.vector.tensor_tensor(fresh[:], act["i"][:], act["u"][:], MULT)
-        c_sb = held.tile([H, N], F32, name="c_sb")
-        nc.vector.tensor_tensor(c_sb[:], kept[:], fresh[:], ADD)
-        tanh_c = held.tile([H, N], F32, name="tanh_c")
-        nc.scalar.activation(tanh_c[:], c_sb[:], TANH)
-        out_sb = held.tile([H, N], F32, name="out_sb")
-        nc.vector.tensor_tensor(out_sb[:], act["o"][:], tanh_c[:], MULT)
-        nc.sync.dma_start(out, out_sb[:])
+        for c in range(CHUNKS):
+            tanh_c = work.tile([H, W], F32, name="tanh_c")
+            nc.scalar.activation(tanh_c[:], c_new[c][:], TANH)
+            out_sb = work.tile([H, W], F32, name="out_sb")
+            nc.vector.tensor_tensor(out_sb[:], act_o[c][:], tanh_c[:], MULT)
+            nc.sync.dma_start(out[:, c * W : (c + 1) * W], out_sb[:])

@@ -1,3 +1,4 @@
+import concourse.masks as masks
 import concourse.mybir as mybir
 
 BF16, F32, U16 = mybir.dt.bfloat16, mybir.dt.float32, mybir.dt.uint16
@@ -27,15 +28,16 @@ def tile_arrdecodermodel_kernel(
         tc.psum_pool(name="psum", bufs=PSUM_BANKS) as psum,
     ):
         zeros = held.tile([H, H], BF16, name="zeros")
-        nc.gpsimd.memset(zeros[:], 0.0)
+        nc.vector.memset(zeros[:], 0.0)
         scratch = held.tile([H, 1], F32, name="scratch")
-        nc.gpsimd.memset(scratch[:], 0.0)
+        nc.vector.memset(scratch[:], 0.0)
 
-        b_in_sb = held.tile([H, 1], F32, name="b_in_sb")
-        nc.scalar.dma_start(b_in_sb[:], b_in)
-        b_lstm_sb = held.tile([H, 4], F32, name="b_lstm_sb")
-        with nc.allow_non_contiguous_dma(reason="512 bias values, one to a partition and gate"):
-            nc.gpsimd.dma_start(b_lstm_sb[:], b_lstm.rearrange("(g p) one -> p (g one)", p=H))
+        b_in_row = held.tile([1, H], F32, name="b_in_row")
+        nc.scalar.dma_start(b_in_row[:], b_in.rearrange("p one -> one p"))
+        b_lstm_rows = held.tile([4, H], F32, name="b_lstm_rows")
+        nc.gpsimd.dma_start(b_lstm_rows[:], b_lstm.rearrange("(g p) one -> g (p one)", p=H))
+        identity = held.tile([4, 4], F32, name="identity")
+        masks.make_identity(nc, identity[:])
 
         warm_ps = psum.tile([H, H], F32, name="warm_ps", tag="bank")
         for w in range(WARM_MATMULS):
@@ -63,6 +65,11 @@ def tile_arrdecodermodel_kernel(
             nc.sync.dma_start(h_prev_sb[c][:], h_prev[:, c * W : (c + 1) * W])
         nc.sync.dma_start(c_prev_sb[:], c_prev)
 
+        b_in_ps = psum.tile([H, 2], F32, name="b_in_ps", tag="bank")
+        nc.tensor.matmul(b_in_ps[:], b_in_row[:], identity[0:1, 0:2], start=True, stop=True)
+        b_in_sb = held.tile([H, 1], F32, name="b_in_sb")
+        nc.vector.tensor_copy(b_in_sb[:], b_in_ps[:, 0:1])
+
         x_sb = []
         for c in range(CHUNKS):
             x_ps = psum.tile([H, W], F32, name="x_ps", tag="bank")
@@ -72,6 +79,11 @@ def tile_arrdecodermodel_kernel(
             )
             x_sb.append(work.tile([H, W], BF16, name="x_sb"))
             nc.vector.scalar_tensor_tensor(x_sb[c][:], x_ps[:], b_in_sb[:], ctx_sb[c][:], ADD, ADD)
+
+        b_lstm_ps = psum.tile([H, 4], F32, name="b_lstm_ps", tag="bank")
+        nc.tensor.matmul(b_lstm_ps[:], b_lstm_rows[:], identity[:], start=True, stop=True)
+        b_lstm_sb = held.tile([H, 4], F32, name="b_lstm_sb")
+        nc.scalar.copy(b_lstm_sb[:], b_lstm_ps[:])
 
         act_o = []
         c_new = []

@@ -1,4 +1,3 @@
-import concourse.masks as masks
 import concourse.mybir as mybir
 
 BF16, F32, U16 = mybir.dt.bfloat16, mybir.dt.float32, mybir.dt.uint16
@@ -11,6 +10,8 @@ S = 1024
 N = 512
 CHUNKS = 2
 W = N // CHUNKS
+OFFSET_COLUMNS = W // 16
+HALVES = [slice(0, W // 2), slice(W // 2, W)]
 GATES = ("i", "f", "u", "o")
 PSUM_BANKS = 8
 WARM_MATMULS = 16
@@ -28,19 +29,18 @@ def tile_arrdecodermodel_kernel(
         tc.psum_pool(name="psum", bufs=PSUM_BANKS) as psum,
     ):
         zeros = held.tile([H, H], BF16, name="zeros")
-        nc.vector.memset(zeros[:], 0.0)
+        nc.gpsimd.memset(zeros[:], 0.0)
         scratch = held.tile([H, 1], F32, name="scratch")
-        nc.vector.memset(scratch[:], 0.0)
+        nc.gpsimd.memset(scratch[:], 0.0)
 
-        b_in_row = held.tile([1, H], F32, name="b_in_row")
-        nc.scalar.dma_start(b_in_row[:], b_in.rearrange("p one -> one p"))
-        b_lstm_rows = held.tile([4, H], F32, name="b_lstm_rows")
-        nc.gpsimd.dma_start(b_lstm_rows[:], b_lstm.rearrange("(g p) one -> g (p one)", p=H))
-        identity = held.tile([4, 4], F32, name="identity")
-        masks.make_identity(nc, identity[:])
+        b_in_sb = held.tile([H, 1], F32, name="b_in_sb")
+        nc.scalar.dma_start(b_in_sb[:], b_in)
+        b_lstm_sb = held.tile([H, 4], F32, name="b_lstm_sb")
+        with nc.allow_non_contiguous_dma(reason="512 bias values, one to a partition and gate"):
+            nc.gpsimd.dma_start(b_lstm_sb[:], b_lstm.rearrange("(g p) one -> p (g one)", p=H))
 
         warm_ps = psum.tile([H, H], F32, name="warm_ps", tag="bank")
-        for w in range(WARM_MATMULS):
+        for repeat in range(WARM_MATMULS):
             nc.tensor.matmul(warm_ps[:], zeros[:], zeros[:], start=True, stop=True)
 
         nc.scalar.activation(scratch[:], scratch[:], SIGMOID)
@@ -51,8 +51,8 @@ def tile_arrdecodermodel_kernel(
         nc.sync.dma_start(w_emb_sb[:], w_emb)
         table_sb = held.tile([H, S], BF16, name="table_sb")
         nc.sync.dma_start(table_sb[:], table)
-        ctx_sb = [held.tile([H, W], F32, name=f"ctx_sb{c}") for c in range(CHUNKS)]
-        h_prev_sb = [held.tile([H, W], BF16, name=f"h_prev_sb{c}") for c in range(CHUNKS)]
+        ctx_sb = [held.tile([H, W], F32, name=f"ctx_sb{k}") for k in range(CHUNKS)]
+        h_prev_sb = [held.tile([H, W], BF16, name=f"h_prev_sb{k}") for k in range(CHUNKS)]
         w_hh_sb = held.tile([H, 4 * H], BF16, name="w_hh_sb")
         w_ih_sb = held.tile([H, 4 * H], BF16, name="w_ih_sb")
         c_prev_sb = held.tile([H, N], F32, name="c_prev_sb")
@@ -60,45 +60,35 @@ def tile_arrdecodermodel_kernel(
         nc.sync.dma_start(h_prev_sb[0][:], h_prev[:, 0:W])
         nc.sync.dma_start(w_hh_sb[:], w_hh)
         nc.sync.dma_start(w_ih_sb[:], w_ih)
-        for c in range(1, CHUNKS):
-            nc.sync.dma_start(ctx_sb[c][:], ctx[:, c * W : (c + 1) * W])
-            nc.sync.dma_start(h_prev_sb[c][:], h_prev[:, c * W : (c + 1) * W])
+        for k in range(1, CHUNKS):
+            nc.sync.dma_start(ctx_sb[k][:], ctx[:, k * W : (k + 1) * W])
+            nc.sync.dma_start(h_prev_sb[k][:], h_prev[:, k * W : (k + 1) * W])
         nc.sync.dma_start(c_prev_sb[:], c_prev)
 
-        b_in_ps = psum.tile([H, 2], F32, name="b_in_ps", tag="bank")
-        nc.tensor.matmul(b_in_ps[:], b_in_row[:], identity[0:1, 0:2], start=True, stop=True)
-        b_in_sb = held.tile([H, 1], F32, name="b_in_sb")
-        nc.vector.tensor_copy(b_in_sb[:], b_in_ps[:, 0:1])
-
         x_sb = []
-        for c in range(CHUNKS):
+        for k in range(CHUNKS):
             x_ps = psum.tile([H, W], F32, name="x_ps", tag="bank")
-            piece = offsets[:, c * (W // 16) : (c + 1) * (W // 16)]
+            piece = offsets[:, k * OFFSET_COLUMNS : (k + 1) * OFFSET_COLUMNS]
             nc.tensor.matmul(
                 x_ps[:], w_emb_sb[:], table_sb[:].indirect(piece), start=True, stop=True
             )
             x_sb.append(work.tile([H, W], BF16, name="x_sb"))
-            nc.vector.scalar_tensor_tensor(x_sb[c][:], x_ps[:], b_in_sb[:], ctx_sb[c][:], ADD, ADD)
-
-        b_lstm_ps = psum.tile([H, 4], F32, name="b_lstm_ps", tag="bank")
-        nc.tensor.matmul(b_lstm_ps[:], b_lstm_rows[:], identity[:], start=True, stop=True)
-        b_lstm_sb = held.tile([H, 4], F32, name="b_lstm_sb")
-        nc.scalar.copy(b_lstm_sb[:], b_lstm_ps[:])
+            nc.vector.scalar_tensor_tensor(x_sb[k][:], x_ps[:], b_in_sb[:], ctx_sb[k][:], ADD, ADD)
 
         act_o = []
         c_new = []
-        for c in range(CHUNKS):
+        for k in range(CHUNKS):
             z_ps = {}
             for g, gate in enumerate(GATES):
                 z_ps[gate] = psum.tile([H, W], F32, name=f"z_{gate}", tag="bank")
                 nc.tensor.matmul(
-                    z_ps[gate][:], w_hh_sb[:, g * H : (g + 1) * H], h_prev_sb[c][:],
+                    z_ps[gate][:], w_hh_sb[:, g * H : (g + 1) * H], h_prev_sb[k][:],
                     start=True, stop=False,
                 )
             act = {}
             for g, gate in enumerate(GATES):
                 nc.tensor.matmul(
-                    z_ps[gate][:], w_ih_sb[:, g * H : (g + 1) * H], x_sb[c][:],
+                    z_ps[gate][:], w_ih_sb[:, g * H : (g + 1) * H], x_sb[k][:],
                     start=False, stop=True,
                 )
                 act[gate] = work.tile([H, W], F32, name=f"act_{gate}")
@@ -106,17 +96,23 @@ def tile_arrdecodermodel_kernel(
                     act[gate][:], z_ps[gate][:], TANH if gate == "u" else SIGMOID,
                     bias=b_lstm_sb[:, g : g + 1],
                 )
+            c_prev_k = c_prev_sb[:, k * W : (k + 1) * W]
             kept = work.tile([H, W], F32, name="kept")
-            nc.vector.tensor_tensor(kept[:], act["f"][:], c_prev_sb[:, c * W : (c + 1) * W], MULT)
+            for half in HALVES:
+                nc.vector.tensor_tensor(kept[:, half], act["f"][:, half], c_prev_k[:, half], MULT)
             fresh = work.tile([H, W], F32, name="fresh")
-            nc.vector.tensor_tensor(fresh[:], act["i"][:], act["u"][:], MULT)
+            for half in HALVES:
+                nc.vector.tensor_tensor(fresh[:, half], act["i"][:, half], act["u"][:, half], MULT)
             c_new.append(work.tile([H, W], F32, name="c_new"))
-            nc.vector.tensor_tensor(c_new[c][:], kept[:], fresh[:], ADD)
+            for half in HALVES:
+                nc.vector.tensor_tensor(c_new[k][:, half], kept[:, half], fresh[:, half], ADD)
             act_o.append(act["o"])
 
-        for c in range(CHUNKS):
+        for k in range(CHUNKS):
             tanh_c = work.tile([H, W], F32, name="tanh_c")
-            nc.scalar.activation(tanh_c[:], c_new[c][:], TANH)
+            for half in HALVES:
+                nc.scalar.activation(tanh_c[:, half], c_new[k][:, half], TANH)
             out_sb = work.tile([H, W], F32, name="out_sb")
-            nc.vector.tensor_tensor(out_sb[:], act_o[c][:], tanh_c[:], MULT)
-            nc.sync.dma_start(out[:, c * W : (c + 1) * W], out_sb[:])
+            for half in HALVES:
+                nc.vector.tensor_tensor(out_sb[:, half], act_o[k][:, half], tanh_c[:, half], MULT)
+            nc.sync.dma_start(out[:, k * W : (k + 1) * W], out_sb[:])

@@ -10,13 +10,15 @@ S = 1024
 N = 512
 CHUNKS = 2
 W = N // CHUNKS
-OFFSET_COLUMNS = W // 16
+OFFSETS_A_COLUMN = 16
 HALVES = [slice(0, W // 2), slice(W // 2, W)]
+OFFSET_COLUMNS = (W // 2) // OFFSETS_A_COLUMN
 GATES = ("i", "f", "u", "o")
+Q = len(GATES) * H
 PSUM_BANKS = 8
 WARM_MATMULS = 16
 
-FLOPS = 2 * H * H * N + 2 * 2 * H * (4 * H) * N
+FLOPS = 2 * H * H * N + 2 * (2 * H * Q * N)
 
 
 def tile_arrdecodermodel_kernel(
@@ -35,7 +37,7 @@ def tile_arrdecodermodel_kernel(
 
         b_in_sb = held.tile([H, 1], F32, name="b_in_sb")
         nc.scalar.dma_start(b_in_sb[:], b_in)
-        b_lstm_sb = held.tile([H, 4], F32, name="b_lstm_sb")
+        b_lstm_sb = held.tile([H, len(GATES)], F32, name="b_lstm_sb")
         with nc.allow_non_contiguous_dma(reason="512 bias values, one to a partition and gate"):
             nc.gpsimd.dma_start(b_lstm_sb[:], b_lstm.rearrange("(g p) one -> p (g one)", p=H))
 
@@ -45,7 +47,7 @@ def tile_arrdecodermodel_kernel(
 
         nc.scalar.activation(scratch[:], scratch[:], SIGMOID)
 
-        offsets = held.tile([H, N // 16], U16, name="offsets")
+        offsets = held.tile([H, N // OFFSETS_A_COLUMN], U16, name="offsets")
         nc.sync.dma_start(offsets[:], offs)
         w_emb_sb = held.tile([H, H], BF16, name="w_emb_sb")
         nc.sync.dma_start(w_emb_sb[:], w_emb)
@@ -53,8 +55,8 @@ def tile_arrdecodermodel_kernel(
         nc.sync.dma_start(table_sb[:], table)
         ctx_sb = [held.tile([H, W], F32, name=f"ctx_sb{k}") for k in range(CHUNKS)]
         h_prev_sb = [held.tile([H, W], BF16, name=f"h_prev_sb{k}") for k in range(CHUNKS)]
-        w_hh_sb = held.tile([H, 4 * H], BF16, name="w_hh_sb")
-        w_ih_sb = held.tile([H, 4 * H], BF16, name="w_ih_sb")
+        w_hh_sb = held.tile([H, Q], BF16, name="w_hh_sb")
+        w_ih_sb = held.tile([H, Q], BF16, name="w_ih_sb")
         c_prev_sb = held.tile([H, N], F32, name="c_prev_sb")
         nc.sync.dma_start(ctx_sb[0][:], ctx[:, 0:W])
         nc.sync.dma_start(h_prev_sb[0][:], h_prev[:, 0:W])
@@ -67,13 +69,17 @@ def tile_arrdecodermodel_kernel(
 
         x_sb = []
         for k in range(CHUNKS):
-            x_ps = psum.tile([H, W], F32, name="x_ps", tag="bank")
-            piece = offsets[:, k * OFFSET_COLUMNS : (k + 1) * OFFSET_COLUMNS]
-            nc.tensor.matmul(
-                x_ps[:], w_emb_sb[:], table_sb[:].indirect(piece), start=True, stop=True
-            )
             x_sb.append(work.tile([H, W], BF16, name="x_sb"))
-            nc.vector.scalar_tensor_tensor(x_sb[k][:], x_ps[:], b_in_sb[:], ctx_sb[k][:], ADD, ADD)
+            for s, half in enumerate(HALVES):
+                x_ps = psum.tile([H, W // 2], F32, name="x_ps", tag="bank")
+                first = (k * len(HALVES) + s) * OFFSET_COLUMNS
+                piece = offsets[:, first : first + OFFSET_COLUMNS]
+                nc.tensor.matmul(
+                    x_ps[:], w_emb_sb[:], table_sb[:].indirect(piece), start=True, stop=True
+                )
+                nc.vector.scalar_tensor_tensor(
+                    x_sb[k][:, half], x_ps[:], b_in_sb[:], ctx_sb[k][:, half], ADD, ADD
+                )
 
         act_o = []
         c_new = []

@@ -11,8 +11,9 @@ N = 512
 CHUNKS = 2
 W = N // CHUNKS
 OFFSETS_A_COLUMN = 16
-HALVES = [slice(0, W // 2), slice(W // 2, W)]
-OFFSET_COLUMNS = (W // 2) // OFFSETS_A_COLUMN
+OFFSET_COLUMNS = W // OFFSETS_A_COLUMN
+PIECE = 64
+PIECES = [slice(first, first + PIECE) for first in range(0, W, PIECE)]
 GATES = ("i", "f", "u", "o")
 Q = len(GATES) * H
 PSUM_BANKS = 8
@@ -69,17 +70,13 @@ def tile_arrdecodermodel_kernel(
 
         x_sb = []
         for k in range(CHUNKS):
+            x_ps = psum.tile([H, W], F32, name="x_ps", tag="bank")
+            entries = offsets[:, k * OFFSET_COLUMNS : (k + 1) * OFFSET_COLUMNS]
+            nc.tensor.matmul(
+                x_ps[:], w_emb_sb[:], table_sb[:].indirect(entries), start=True, stop=True
+            )
             x_sb.append(work.tile([H, W], BF16, name="x_sb"))
-            for s, half in enumerate(HALVES):
-                x_ps = psum.tile([H, W // 2], F32, name="x_ps", tag="bank")
-                first = (k * len(HALVES) + s) * OFFSET_COLUMNS
-                piece = offsets[:, first : first + OFFSET_COLUMNS]
-                nc.tensor.matmul(
-                    x_ps[:], w_emb_sb[:], table_sb[:].indirect(piece), start=True, stop=True
-                )
-                nc.vector.scalar_tensor_tensor(
-                    x_sb[k][:, half], x_ps[:], b_in_sb[:], ctx_sb[k][:, half], ADD, ADD
-                )
+            nc.vector.scalar_tensor_tensor(x_sb[k][:], x_ps[:], b_in_sb[:], ctx_sb[k][:], ADD, ADD)
 
         act_o = []
         c_new = []
@@ -104,21 +101,21 @@ def tile_arrdecodermodel_kernel(
                 )
             c_prev_k = c_prev_sb[:, k * W : (k + 1) * W]
             kept = work.tile([H, W], F32, name="kept")
-            for half in HALVES:
-                nc.vector.tensor_tensor(kept[:, half], act["f"][:, half], c_prev_k[:, half], MULT)
+            for piece in PIECES:
+                nc.vector.tensor_tensor(kept[:, piece], act["f"][:, piece], c_prev_k[:, piece], MULT)
             fresh = work.tile([H, W], F32, name="fresh")
-            for half in HALVES:
-                nc.vector.tensor_tensor(fresh[:, half], act["i"][:, half], act["u"][:, half], MULT)
+            for piece in PIECES:
+                nc.vector.tensor_tensor(fresh[:, piece], act["i"][:, piece], act["u"][:, piece], MULT)
             c_new.append(work.tile([H, W], F32, name="c_new"))
-            for half in HALVES:
-                nc.vector.tensor_tensor(c_new[k][:, half], kept[:, half], fresh[:, half], ADD)
+            for piece in PIECES:
+                nc.vector.tensor_tensor(c_new[k][:, piece], kept[:, piece], fresh[:, piece], ADD)
             act_o.append(act["o"])
 
         for k in range(CHUNKS):
             tanh_c = work.tile([H, W], F32, name="tanh_c")
-            for half in HALVES:
-                nc.scalar.activation(tanh_c[:, half], c_new[k][:, half], TANH)
+            for piece in PIECES:
+                nc.scalar.activation(tanh_c[:, piece], c_new[k][:, piece], TANH)
             out_sb = work.tile([H, W], F32, name="out_sb")
-            for half in HALVES:
-                nc.vector.tensor_tensor(out_sb[:, half], act_o[k][:, half], tanh_c[:, half], MULT)
+            for piece in PIECES:
+                nc.vector.tensor_tensor(out_sb[:, piece], act_o[k][:, piece], tanh_c[:, piece], MULT)
             nc.sync.dma_start(out[:, k * W : (k + 1) * W], out_sb[:])

@@ -40,7 +40,7 @@ def tile_arrdecodermodel_kernel(
         nc.scalar.dma_start(b_in_sb[:], b_in)
         b_lstm_sb = held.tile([H, len(GATES)], F32, name="b_lstm_sb")
         with nc.allow_non_contiguous_dma(reason="512 bias values, one to a partition and gate"):
-            nc.gpsimd.dma_start(b_lstm_sb[:], b_lstm.rearrange("(g p) one -> p (g one)", p=H))
+            nc.scalar.dma_start(b_lstm_sb[:], b_lstm.rearrange("(g p) one -> p (g one)", p=H))
 
         warm_ps = psum.tile([H, H], F32, name="warm_ps", tag="bank")
         for repeat in range(WARM_MATMULS):

@@ -78,18 +78,18 @@ def tile_arrdecodermodel_kernel(
             x_sb.append(work.tile([H, W], BF16, name="x_sb"))
             nc.vector.scalar_tensor_tensor(x_sb[k][:], x_ps[:], b_in_sb[:], ctx_sb[k][:], ADD, ADD)
 
-        act_o = []
-        c_new = []
-        for k in range(CHUNKS):
+        def gates(k, names):
             z_ps = {}
-            for g, gate in enumerate(GATES):
+            for gate in names:
+                g = GATES.index(gate)
                 z_ps[gate] = psum.tile([H, W], F32, name=f"z_{gate}", tag="bank")
                 nc.tensor.matmul(
                     z_ps[gate][:], w_hh_sb[:, g * H : (g + 1) * H], h_prev_sb[k][:],
                     start=True, stop=False,
                 )
             act = {}
-            for g, gate in enumerate(GATES):
+            for gate in names:
+                g = GATES.index(gate)
                 nc.tensor.matmul(
                     z_ps[gate][:], w_ih_sb[:, g * H : (g + 1) * H], x_sb[k][:],
                     start=False, stop=True,
@@ -99,6 +99,11 @@ def tile_arrdecodermodel_kernel(
                     act[gate][:], z_ps[gate][:], TANH if gate == "u" else SIGMOID,
                     bias=b_lstm_sb[:, g : g + 1],
                 )
+            return act
+
+        c_new = []
+        for k in range(CHUNKS):
+            act = gates(k, ("i", "f", "u"))
             c_prev_k = c_prev_sb[:, k * W : (k + 1) * W]
             kept = work.tile([H, W], F32, name="kept")
             for piece in PIECES:
@@ -109,13 +114,13 @@ def tile_arrdecodermodel_kernel(
             c_new.append(work.tile([H, W], F32, name="c_new"))
             for piece in PIECES:
                 nc.vector.tensor_tensor(c_new[k][:, piece], kept[:, piece], fresh[:, piece], ADD)
-            act_o.append(act["o"])
 
         for k in range(CHUNKS):
+            act_o = gates(k, ("o",))["o"]
             tanh_c = work.tile([H, W], F32, name="tanh_c")
             for piece in PIECES:
                 nc.scalar.activation(tanh_c[:, piece], c_new[k][:, piece], TANH)
             out_sb = work.tile([H, W], F32, name="out_sb")
             for piece in PIECES:
-                nc.vector.tensor_tensor(out_sb[:, piece], act_o[k][:, piece], tanh_c[:, piece], MULT)
+                nc.vector.tensor_tensor(out_sb[:, piece], act_o[:, piece], tanh_c[:, piece], MULT)
             nc.sync.dma_start(out[:, k * W : (k + 1) * W], out_sb[:])

@@ -36,6 +36,11 @@ def tile_arrdecodermodel_kernel(
         scratch = held.tile([H, 1], F32, name="scratch")
         nc.gpsimd.memset(scratch[:], 0.0)
 
+        offsets = held.tile([H, N // OFFSETS_A_COLUMN], U16, name="offsets")
+        nc.sync.dma_start(offsets[:], offs)
+        w_emb_sb = held.tile([H, H], BF16, name="w_emb_sb")
+        nc.sync.dma_start(w_emb_sb[:], w_emb)
+
         b_in_sb = held.tile([H, 1], F32, name="b_in_sb")
         nc.scalar.dma_start(b_in_sb[:], b_in)
         b_lstm_sb = held.tile([H, len(GATES)], F32, name="b_lstm_sb")
@@ -48,10 +53,6 @@ def tile_arrdecodermodel_kernel(
 
         nc.scalar.activation(scratch[:], scratch[:], SIGMOID)
 
-        offsets = held.tile([H, N // OFFSETS_A_COLUMN], U16, name="offsets")
-        nc.sync.dma_start(offsets[:], offs)
-        w_emb_sb = held.tile([H, H], BF16, name="w_emb_sb")
-        nc.sync.dma_start(w_emb_sb[:], w_emb)
         table_sb = held.tile([H, S], BF16, name="table_sb")
         nc.sync.dma_start(table_sb[:], table)
         ctx_sb = [held.tile([H, W], F32, name=f"ctx_sb{k}") for k in range(CHUNKS)]

@@ -33,8 +33,6 @@ def tile_arrdecodermodel_kernel(
     ):
         zeros = held.tile([H, H], BF16, name="zeros")
         nc.gpsimd.memset(zeros[:], 0.0)
-        scratch = held.tile([H, 1], F32, name="scratch")
-        nc.gpsimd.memset(scratch[:], 0.0)
 
         offsets = held.tile([H, N // OFFSETS_A_COLUMN], U16, name="offsets")
         nc.sync.dma_start(offsets[:], offs)
@@ -50,8 +48,6 @@ def tile_arrdecodermodel_kernel(
         warm_ps = psum.tile([H, H], F32, name="warm_ps", tag="bank")
         for repeat in range(WARM_MATMULS):
             nc.tensor.matmul(warm_ps[:], zeros[:], zeros[:], start=True, stop=True)
-
-        nc.scalar.activation(scratch[:], scratch[:], SIGMOID)
 
         table_sb = held.tile([H, S], BF16, name="table_sb")
         nc.sync.dma_start(table_sb[:], table)

@@ -14,6 +14,8 @@ OFFSETS_A_COLUMN = 16
 OFFSET_COLUMNS = W // OFFSETS_A_COLUMN
 PIECE = 64
 PIECES = [slice(first, first + PIECE) for first in range(0, W, PIECE)]
+WHOLE = [slice(0, W)]
+HALVES = [slice(0, W // 2), slice(W // 2, W)]
 GATES = ("i", "f", "u", "o")
 Q = len(GATES) * H
 PSUM_BANKS = 8
@@ -92,19 +94,19 @@ def tile_arrdecodermodel_kernel(
                     start=False, stop=True,
                 )
                 act[gate] = work.tile([H, W], F32, name=f"act_{gate}")
-                nc.scalar.activation(
-                    act[gate][:], z_ps[gate][:], TANH if gate == "u" else SIGMOID,
-                    bias=b_lstm_sb[:, g : g + 1],
-                )
+                for part in HALVES if gate == "u" else WHOLE:
+                    nc.scalar.activation(
+                        act[gate][:, part], z_ps[gate][:, part], TANH if gate == "u" else SIGMOID,
+                        bias=b_lstm_sb[:, g : g + 1],
+                    )
             return act
 
         c_new = []
         for k in range(CHUNKS):
-            act = gates(k, ("i", "f", "u"))
+            act = gates(k, ("f", "i", "u"))
             c_prev_k = c_prev_sb[:, k * W : (k + 1) * W]
             kept = work.tile([H, W], F32, name="kept")
-            for piece in PIECES:
-                nc.vector.tensor_tensor(kept[:, piece], act["f"][:, piece], c_prev_k[:, piece], MULT)
+            nc.vector.tensor_tensor(kept[:], act["f"][:], c_prev_k, MULT)
             fresh = work.tile([H, W], F32, name="fresh")
             for piece in PIECES:
                 nc.vector.tensor_tensor(fresh[:, piece], act["i"][:, piece], act["u"][:, piece], MULT)

@@ -12,10 +12,9 @@ CHUNKS = 2
 W = N // CHUNKS
 OFFSETS_A_COLUMN = 16
 OFFSET_COLUMNS = W // OFFSETS_A_COLUMN
-PIECE = 64
-PIECES = [slice(first, first + PIECE) for first in range(0, W, PIECE)]
 WHOLE = [slice(0, W)]
 HALVES = [slice(0, W // 2), slice(W // 2, W)]
+PIECES = [HALVES, [slice(first, first + 64) for first in range(0, W, 64)]]
 GATES = ("i", "f", "u", "o")
 Q = len(GATES) * H
 PSUM_BANKS = 8
@@ -108,18 +107,18 @@ def tile_arrdecodermodel_kernel(
             kept = work.tile([H, W], F32, name="kept")
             nc.vector.tensor_tensor(kept[:], act["f"][:], c_prev_k, MULT)
             fresh = work.tile([H, W], F32, name="fresh")
-            for piece in PIECES:
+            for piece in PIECES[k]:
                 nc.vector.tensor_tensor(fresh[:, piece], act["i"][:, piece], act["u"][:, piece], MULT)
             c_new.append(work.tile([H, W], F32, name="c_new"))
-            for piece in PIECES:
+            for piece in PIECES[k]:
                 nc.vector.tensor_tensor(c_new[k][:, piece], kept[:, piece], fresh[:, piece], ADD)
 
+        act_o = [gates(k, ("o",))["o"] for k in range(CHUNKS)]
         for k in range(CHUNKS):
-            act_o = gates(k, ("o",))["o"]
             tanh_c = work.tile([H, W], F32, name="tanh_c")
-            for piece in PIECES:
+            for piece in PIECES[k]:
                 nc.scalar.activation(tanh_c[:, piece], c_new[k][:, piece], TANH)
             out_sb = work.tile([H, W], F32, name="out_sb")
-            for piece in PIECES:
-                nc.vector.tensor_tensor(out_sb[:, piece], act_o[:, piece], tanh_c[:, piece], MULT)
+            for piece in PIECES[k]:
+                nc.vector.tensor_tensor(out_sb[:, piece], act_o[k][:, piece], tanh_c[:, piece], MULT)
             nc.sync.dma_start(out[:, k * W : (k + 1) * W], out_sb[:])

@@ -11,10 +11,10 @@ N = 512
 CHUNKS = 2
 W = N // CHUNKS
 OFFSETS_A_COLUMN = 16
-OFFSET_COLUMNS = W // OFFSETS_A_COLUMN
 WHOLE = [slice(0, W)]
 HALVES = [slice(0, W // 2), slice(W // 2, W)]
 PIECES = [HALVES, [slice(first, first + 64) for first in range(0, W, 64)]]
+X_PARTS = [HALVES, WHOLE]
 GATES = ("i", "f", "u", "o")
 Q = len(GATES) * H
 PSUM_BANKS = 8
@@ -68,35 +68,43 @@ def tile_arrdecodermodel_kernel(
 
         x_sb = []
         for k in range(CHUNKS):
-            x_ps = psum.tile([H, W], F32, name="x_ps", tag="bank")
-            entries = offsets[:, k * OFFSET_COLUMNS : (k + 1) * OFFSET_COLUMNS]
-            nc.tensor.matmul(
-                x_ps[:], w_emb_sb[:], table_sb[:].indirect(entries), start=True, stop=True
-            )
             x_sb.append(work.tile([H, W], BF16, name="x_sb"))
-            nc.vector.scalar_tensor_tensor(x_sb[k][:], x_ps[:], b_in_sb[:], ctx_sb[k][:], ADD, ADD)
+            for part in X_PARTS[k]:
+                x_ps = psum.tile([H, part.stop - part.start], F32, name="x_ps", tag="bank")
+                first, last = k * W + part.start, k * W + part.stop
+                entries = offsets[:, first // OFFSETS_A_COLUMN : last // OFFSETS_A_COLUMN]
+                nc.tensor.matmul(
+                    x_ps[:], w_emb_sb[:], table_sb[:].indirect(entries), start=True, stop=True
+                )
+                nc.vector.scalar_tensor_tensor(
+                    x_sb[k][:, part], x_ps[:], b_in_sb[:], ctx_sb[k][:, part], ADD, ADD
+                )
 
         def gates(k, names):
-            z_ps = {}
-            for gate in names:
+            act = {gate: work.tile([H, W], F32, name=f"act_{gate}") for gate in names}
+            units = [(gate, part) for gate in names for part in (X_PARTS[k] if gate == "f" else WHOLE)]
+            z_ps = []
+            for gate, part in units:
                 g = GATES.index(gate)
-                z_ps[gate] = psum.tile([H, W], F32, name=f"z_{gate}", tag="bank")
+                z_ps.append(psum.tile([H, part.stop - part.start], F32, name="z_ps", tag="bank"))
                 nc.tensor.matmul(
-                    z_ps[gate][:], w_hh_sb[:, g * H : (g + 1) * H], h_prev_sb[k][:],
+                    z_ps[-1][:], w_hh_sb[:, g * H : (g + 1) * H], h_prev_sb[k][:, part],
                     start=True, stop=False,
                 )
-            act = {}
-            for gate in names:
+            for z, (gate, part) in zip(z_ps, units):
                 g = GATES.index(gate)
                 nc.tensor.matmul(
-                    z_ps[gate][:], w_ih_sb[:, g * H : (g + 1) * H], x_sb[k][:],
+                    z[:], w_ih_sb[:, g * H : (g + 1) * H], x_sb[k][:, part],
                     start=False, stop=True,
                 )
-                act[gate] = work.tile([H, W], F32, name=f"act_{gate}")
-                for part in HALVES if gate == "u" else WHOLE:
+                if gate == "u":
+                    for half in HALVES:
+                        nc.scalar.activation(
+                            act[gate][:, half], z[:, half], TANH, bias=b_lstm_sb[:, g : g + 1]
+                        )
+                else:
                     nc.scalar.activation(
-                        act[gate][:, part], z_ps[gate][:, part], TANH if gate == "u" else SIGMOID,
-                        bias=b_lstm_sb[:, g : g + 1],
+                        act[gate][:, part], z[:], SIGMOID, bias=b_lstm_sb[:, g : g + 1]
                     )
             return act
 

import concourse.mybir as mybir

BF16, F32, U16 = mybir.dt.bfloat16, mybir.dt.float32, mybir.dt.uint16
ADD, MULT = mybir.AluOpType.add, mybir.AluOpType.mult
SIGMOID = mybir.ActivationFunctionType.Sigmoid
TANH = mybir.ActivationFunctionType.Tanh

H = 128
S = 1024
N = 512
CHUNKS = 2
W = N // CHUNKS
OFFSETS_A_COLUMN = 16
WHOLE = [slice(0, W)]
HALVES = [slice(0, W // 2), slice(W // 2, W)]
PIECES = [HALVES, [slice(first, first + 64) for first in range(0, W, 64)]]
X_PARTS = [HALVES, WHOLE]
GATES = ("i", "f", "u", "o")
Q = len(GATES) * H
PSUM_BANKS = 8
WARM_MATMULS = 16

FLOPS = 2 * H * H * N + 2 * (2 * H * Q * N)


def tile_arrdecodermodel_kernel(
    tc, table, w_emb, ctx, b_in, w_ih, w_hh, h_prev, c_prev, b_lstm, offs, out
):
    nc = tc.nc
    with (
        tc.tile_pool(name="held", bufs=1) as held,
        tc.tile_pool(name="work", bufs=CHUNKS) as work,
        tc.psum_pool(name="psum", bufs=PSUM_BANKS) as psum,
    ):
        zeros = held.tile([H, H], BF16, name="zeros")
        nc.gpsimd.memset(zeros[:], 0.0)

        offsets = held.tile([H, N // OFFSETS_A_COLUMN], U16, name="offsets")
        nc.sync.dma_start(offsets[:], offs)
        w_emb_sb = held.tile([H, H], BF16, name="w_emb_sb")
        nc.sync.dma_start(w_emb_sb[:], w_emb)

        b_in_sb = held.tile([H, 1], F32, name="b_in_sb")
        nc.scalar.dma_start(b_in_sb[:], b_in)
        b_lstm_sb = held.tile([H, len(GATES)], F32, name="b_lstm_sb")
        with nc.allow_non_contiguous_dma(reason="512 bias values, one to a partition and gate"):
            nc.scalar.dma_start(b_lstm_sb[:], b_lstm.rearrange("(g p) one -> p (g one)", p=H))

        warm_ps = psum.tile([H, H], F32, name="warm_ps", tag="bank")
        for repeat in range(WARM_MATMULS):
            nc.tensor.matmul(warm_ps[:], zeros[:], zeros[:], start=True, stop=True)

        table_sb = held.tile([H, S], BF16, name="table_sb")
        nc.sync.dma_start(table_sb[:], table)
        ctx_sb = [held.tile([H, W], F32, name=f"ctx_sb{k}") for k in range(CHUNKS)]
        h_prev_sb = [held.tile([H, W], BF16, name=f"h_prev_sb{k}") for k in range(CHUNKS)]
        w_hh_sb = held.tile([H, Q], BF16, name="w_hh_sb")
        w_ih_sb = held.tile([H, Q], BF16, name="w_ih_sb")
        c_prev_sb = held.tile([H, N], F32, name="c_prev_sb")
        nc.sync.dma_start(ctx_sb[0][:], ctx[:, 0:W])
        nc.sync.dma_start(h_prev_sb[0][:], h_prev[:, 0:W])
        nc.sync.dma_start(w_hh_sb[:], w_hh)
        nc.sync.dma_start(w_ih_sb[:], w_ih)
        for k in range(1, CHUNKS):
            nc.sync.dma_start(ctx_sb[k][:], ctx[:, k * W : (k + 1) * W])
            nc.sync.dma_start(h_prev_sb[k][:], h_prev[:, k * W : (k + 1) * W])
        nc.sync.dma_start(c_prev_sb[:], c_prev)

        x_sb = []
        for k in range(CHUNKS):
            x_sb.append(work.tile([H, W], BF16, name="x_sb"))
            for part in X_PARTS[k]:
                x_ps = psum.tile([H, part.stop - part.start], F32, name="x_ps", tag="bank")
                first, last = k * W + part.start, k * W + part.stop
                entries = offsets[:, first // OFFSETS_A_COLUMN : last // OFFSETS_A_COLUMN]
                nc.tensor.matmul(
                    x_ps[:], w_emb_sb[:], table_sb[:].indirect(entries), start=True, stop=True
                )
                nc.vector.scalar_tensor_tensor(
                    x_sb[k][:, part], x_ps[:], b_in_sb[:], ctx_sb[k][:, part], ADD, ADD
                )

        def gates(k, names):
            act = {gate: work.tile([H, W], F32, name=f"act_{gate}") for gate in names}
            units = [(gate, part) for gate in names for part in (X_PARTS[k] if gate == "f" else WHOLE)]
            z_ps = []
            for gate, part in units:
                g = GATES.index(gate)
                z_ps.append(psum.tile([H, part.stop - part.start], F32, name="z_ps", tag="bank"))
                nc.tensor.matmul(
                    z_ps[-1][:], w_hh_sb[:, g * H : (g + 1) * H], h_prev_sb[k][:, part],
                    start=True, stop=False,
                )
            for z, (gate, part) in zip(z_ps, units):
                g = GATES.index(gate)
                nc.tensor.matmul(
                    z[:], w_ih_sb[:, g * H : (g + 1) * H], x_sb[k][:, part],
                    start=False, stop=True,
                )
                if gate == "u":
                    for half in HALVES:
                        nc.scalar.activation(
                            act[gate][:, half], z[:, half], TANH, bias=b_lstm_sb[:, g : g + 1]
                        )
                else:
                    nc.scalar.activation(
                        act[gate][:, part], z[:], SIGMOID, bias=b_lstm_sb[:, g : g + 1]
                    )
            return act

        c_new = []
        for k in range(CHUNKS):
            act = gates(k, ("f", "i", "u"))
            c_prev_k = c_prev_sb[:, k * W : (k + 1) * W]
            kept = work.tile([H, W], F32, name="kept")
            nc.vector.tensor_tensor(kept[:], act["f"][:], c_prev_k, MULT)
            fresh = work.tile([H, W], F32, name="fresh")
            for piece in PIECES[k]:
                nc.vector.tensor_tensor(fresh[:, piece], act["i"][:, piece], act["u"][:, piece], MULT)
            c_new.append(work.tile([H, W], F32, name="c_new"))
            for piece in PIECES[k]:
                nc.vector.tensor_tensor(c_new[k][:, piece], kept[:, piece], fresh[:, piece], ADD)

        act_o = [gates(k, ("o",))["o"] for k in range(CHUNKS)]
        for k in range(CHUNKS):
            tanh_c = work.tile([H, W], F32, name="tanh_c")
            for piece in PIECES[k]:
                nc.scalar.activation(tanh_c[:, piece], c_new[k][:, piece], TANH)
            out_sb = work.tile([H, W], F32, name="out_sb")
            for piece in PIECES[k]:
                nc.vector.tensor_tensor(out_sb[:, piece], act_o[k][:, piece], tanh_c[:, piece], MULT)
            nc.sync.dma_start(out[:, k * W : (k + 1) * W], out_sb[:])
